import numpy as np
import ml_dtypes


def mxq(x, axis, fmt="e4m3"):
    dtype, down = {"e4m3": (ml_dtypes.float8_e4m3fn, 7), "e5m2": (ml_dtypes.float8_e5m2, 14)}[fmt]
    v = np.moveaxis(np.asarray(x, np.float32).astype(ml_dtypes.bfloat16).astype(np.float64), axis, -1)
    blocks = v.reshape(v.shape[:-1] + (-1, 32))
    amax = np.abs(blocks).max(-1, keepdims=True)
    byte = np.maximum(np.where(amax > 0, np.frexp(amax)[1] - 1 + 127, 0) - down, 1)
    scale = np.exp2(byte - 127.0)
    codes = (blocks / scale).astype(np.float32).astype(dtype).astype(np.float64)
    return np.moveaxis((codes * scale).reshape(v.shape), -1, axis)


WIDE = False


def mx_kscale(k):
    if not WIDE:
        return np.ones(k)
    levels = np.array([10, -10, 5, -5, 0])
    if k % 512:
        return np.exp2(np.random.permutation(np.resize(levels, k // 32))).repeat(32)
    a = np.empty((k // 512, 16))
    for p in range(k // 512):
        a[p, :8] = np.random.permutation(np.resize(levels, 8))
        for g in range(8):
            far = levels[np.abs(levels - a[p, g]) >= 10]
            a[p, g + 8] = far[np.random.randint(len(far))]
    return np.exp2(a.ravel()).repeat(32)


BF16 = ml_dtypes.bfloat16


def bf(x):
    return np.asarray(x, np.float32).astype(BF16)


def f64(x):
    return np.asarray(x).astype(np.float64)


B, S, D, P, N1, N2, N3 = 2, 512, 1024, 128, 3, 2, 3
H = N1 + N2 + N3


def setup_inputs():
    s = mx_kscale(D)
    a = 1.0 / np.sqrt(D)
    return {"x": bf(np.random.standard_normal((B, S, D)) * s),
            "w_now": bf(np.random.standard_normal((H, P, D)) * a / s),
            "w_back1": bf(np.random.standard_normal((N2 + N3, P, D)) * a / s),
            "w_back2": bf(np.random.standard_normal((N3, P, D)) * a / s),
            "bias": bf(np.random.standard_normal((H, P)) * 0.5)}


def reference(x, w_now, w_back1, w_back2, bias):
    xq = mxq(f64(x), 2, "e4m3")
    y = 0.0
    for j, w in enumerate((w_now, w_back1, w_back2)):
        z = xq @ mxq(f64(w), 2, "e4m3").reshape(-1, D).T
        y = y + np.pad(z[:, :S - j], ((0, 0), (j, 0), (H * P - z.shape[-1], 0)))
    return y.reshape(B, S, H, P).transpose(0, 2, 1, 3) + f64(bias)[None, :, None, :]

@@ -1,0 +1,377 @@
+from contextlib import ExitStack
+
+import concourse.mybir as mybir
+from concourse.masks import make_identity
+
+F32 = mybir.dt.float32
+BF16 = mybir.dt.bfloat16
+U32 = mybir.dt.uint32
+U8 = mybir.dt.uint8
+FP8X4 = mybir.dt.float8_e4m3fn_x4
+ADD = mybir.AluOpType.add
+
+B, S, D, P, H = 2, 512, 1024, 128, 8
+R = 4
+G = 2
+FLOPS = 2 * B * S * D * P * 16
+
+
+def tile_multiheadhomogeneousattention_pa_kernel(tc, x, w_now, w_back1, w_back2, bias, out):
+    nc = tc.nc
+    with ExitStack() as ctx:
+        const = ctx.enter_context(tc.tile_pool(name="const", bufs=1))
+        raw = ctx.enter_context(tc.tile_pool(name="raw", bufs=1))
+        grp = ctx.enter_context(tc.tile_pool(name="grp", bufs=1))
+        mxp = ctx.enter_context(tc.tile_pool(name="mxp", bufs=1))
+        outp = ctx.enter_context(tc.tile_pool(name="outp", bufs=1))
+        psum = ctx.enter_context(tc.psum_pool(name="psum", bufs=8))
+        ctx.enter_context(tc.manual_schedule())
+
+        ident = const.tile([P, P], F32, name="ident")
+        ones = const.tile([P, P], BF16, name="ones")
+        bias_in = const.tile([1, H * P], BF16, name="bias_in")
+        bias_row = const.tile([P, H * P], BF16, name="bias_row")
+        bias_all = const.tile([P, H * P], F32, name="bias_all")
+        heads = {"A": 4, "B": 4, "C": 4, "E": 1, "F": 3}
+        w_raw, w_grp, w_code, w_scale = {}, {}, {}, {}
+        for k in ("A", "E", "B", "C", "F"):
+            nh = heads[k]
+            w_raw[k] = raw.tile([P, nh * D], BF16, name="w_raw" + k)
+            w_grp[k] = grp.tile([P, nh * D], BF16, name="w_grp" + k, align_bytes=64)
+            w_code[k] = mxp.tile([P, nh * D // 4], U32, name="w_code" + k, align_bytes=64)
+            w_scale[k] = mxp.tile([P, nh * D // 4], U8, name="w_scale" + k, align_bytes=64)
+        x_raw, x_grp, x_code, x_scale = [], [], [], []
+        s_grp, s_code, s_scale = [], [], []
+        o_sb = []
+        for n in range(B):
+            x_raw.append(raw.tile([P, R * D], BF16, name="x_raw%d" % n))
+            x_grp.append(grp.tile([P, R * D], BF16, name="x_grp%d" % n, align_bytes=64))
+            x_code.append(mxp.tile([P, R * D // 4], U32, name="x_code%d" % n, align_bytes=64))
+            x_scale.append(mxp.tile([P, R * D // 4], U8, name="x_scale%d" % n, align_bytes=64))
+            s_grp.append(grp.tile([P, 2 * D], BF16, name="s_grp%d" % n, align_bytes=64))
+            s_code.append(mxp.tile([P, 2 * D // 4], U32, name="s_code%d" % n, align_bytes=64))
+            s_scale.append(mxp.tile([P, 2 * D // 4], U8, name="s_scale%d" % n, align_bytes=64))
+            o_sb.append([outp.tile([P, 4 * R * P], F32, name="o_sb%d_%d" % (n, hf)) for hf in range(2)])
+
+        def load_w(k, src, h0, h1):
+            nc.sync.dma_start(
+                out=w_raw[k][:, h0 * D:h1 * D].rearrange("p (h d) -> p h d", h=h1 - h0),
+                in_=src.rearrange("h p d -> p h d"),
+            )
+
+        def load_x(n, r0, r1):
+            nc.sync.dma_start(
+                out=x_raw[n][:, r0 * D:r1 * D],
+                in_=x[n].rearrange("(m r) d -> m (r d)", r=R)[:, r0 * D:r1 * D],
+            )
+
+        nc.sync.dma_start(out=bias_in[:], in_=bias.rearrange("(o h) p -> o (h p)", o=1))
+        load_w("A", w_now[0:2], 0, 2)
+        load_w("A", w_now[2:4], 2, 4)
+        load_x(0, 0, 2)
+        load_x(0, 2, 4)
+        load_w("E", w_back1[0:1], 0, 1)
+        load_x(1, 0, 2)
+        load_x(1, 2, 4)
+        load_w("B", w_now[4:6], 0, 2)
+        load_w("B", w_now[6:8], 2, 4)
+        load_w("C", w_back1[1:3], 0, 2)
+        load_w("C", w_back1[3:5], 2, 4)
+        load_w("F", w_back2[0:3], 0, 3)
+
+        make_identity(nc, ident[:])
+        nc.vector.memset(ones[:], 1.0)
+        nc.vector.memset(bias_row[:], 0.0)
+        for n in range(B):
+            nc.vector.memset(s_grp[n][:].bitcast(F32), 0.0)
+        nc.vector.tensor_copy(out=bias_row[0:1, :], in_=bias_in[:])
+        for hf in range(2):
+            bb = psum.tile([P, 512], F32, name="bb", tag="bank")
+            nc.tensor.matmul(bb[:], lhsT=ones[:], rhs=bias_row[:, hf * 512:(hf + 1) * 512], start=True, stop=True)
+            nc.scalar.copy(out=bias_all[:, hf * 512:(hf + 1) * 512], in_=bb[:])
+
+        flipped = {}
+        accs = {}
+
+        def copy_on(eng, dst, src):
+            if eng == "v":
+                nc.vector.tensor_copy(out=dst, in_=src)
+            else:
+                nc.scalar.copy(out=dst, in_=src)
+
+        def flip(words):
+            bank = psum.tile([P, 512], F32, name="bank", tag="bank")
+            for c in range(4):
+                g, u = divmod(c, 2)
+                nc.tensor.transpose(bank[:, c * P:(c + 1) * P], words[:, g * 256 + u:(g + 1) * 256:2], ident[:])
+            return bank[:].rearrange("q (g u m) -> q g m u", g=G, u=2)
+
+        def quant(src, code, scale, c0, c1):
+            nc.vector.quantize_mx(
+                out=code[:, c0 // 4:c1 // 4].bitcast(FP8X4),
+                scales=scale[:, c0 // 4:c1 // 4],
+                in_=src[:, c0:c1],
+            )
+
+        def tw(k, h):
+            flipped[(k, h)] = flip(w_raw[k][:].bitcast(F32)[:, h * 512:(h + 1) * 512])
+
+        def cw(k, h, eng):
+            dst = w_grp[k][:].bitcast(F32).rearrange("q (g h m u) -> q g h m u", g=G, h=heads[k], u=2)
+            copy_on(eng, dst[:, :, h, :, :], flipped[(k, h)])
+
+        def tx(n, r):
+            flipped[(n, r)] = flip(x_raw[n][:].bitcast(F32)[:, r * 512:(r + 1) * 512])
+
+        def cx(n, r, eng):
+            dst = x_grp[n][:].bitcast(F32)[:, r * 512:(r + 1) * 512].rearrange("q (g m u) -> q g m u", g=G, u=2)
+            copy_on(eng, dst, flipped[(n, r)])
+
+        def sh(n, r):
+            nc.vector.tensor_copy(
+                out=s_grp[n][:].rearrange("q (t g c) -> q t g c", t=2, g=G)[:, r - 2, :, 4:512],
+                in_=x_grp[n][:].rearrange("q (t g c) -> q t g c", t=R, g=G)[:, r, :, 0:508],
+            )
+
+        def qw(k, c0, c1):
+            quant(w_grp[k], w_code[k], w_scale[k], c0, c1)
+
+        def qx(n, c0, c1):
+            quant(x_grp[n], x_code[n], x_scale[n], c0, c1)
+
+        def qs(n, c0, c1):
+            quant(s_grp[n], s_code[n], s_scale[n], c0, c1)
+
+        def stat(n, r, j, g):
+            rr = r - j
+            if rr >= 0:
+                c = (rr * G + g) * P
+                return x_code[n][:, c:c + P].bitcast(FP8X4), x_scale[n][:, c:c + P]
+            c = ((rr + 2) * G + g) * P
+            return s_code[n][:, c:c + P].bitcast(FP8X4), s_scale[n][:, c:c + P]
+
+        def mx(n, hf, r, j, g, k, c0, width, o0, start, stop):
+            if start:
+                accs[(n, hf, r)] = psum.tile([P, 512], F32, name="acc", tag="bank")
+            lt, ls = stat(n, r, j, g)
+            nc.tensor.matmul_mx(
+                out=accs[(n, hf, r)][:, o0:o0 + width],
+                lhsT=lt,
+                lhsT_scale=ls,
+                rhs=w_code[k][:, c0:c0 + width].bitcast(FP8X4),
+                rhs_scale=w_scale[k][:, c0:c0 + width],
+                start=start,
+                stop=stop,
+            )
+
+        span = {0: (0, 0, 4), 1: (1, 0, 4), 2: (1, 0, 2), 3: (1, 2, 2)}
+
+        def ev(n, hf, r):
+            hb, h0, nh = span[hf]
+            nc.vector.tensor_tensor(
+                out=o_sb[n][hb][:].rearrange("q (h r p) -> q h r p", h=4, r=R)[:, h0:h0 + nh, r, :],
+                in0=accs[(n, hf, r)][:, h0 * P:(h0 + nh) * P].rearrange("q (h p) -> q h p", h=nh),
+                in1=bias_all[:, (4 * hb + h0) * P:(4 * hb + h0 + nh) * P].rearrange("q (h p) -> q h p", h=nh),
+                op=ADD,
+            )
+
+        def st(n, hf, r0, r1):
+            hb, h0, nh = span[hf]
+            nc.sync.dma_start(
+                out=out[n, 4 * hb + h0:4 * hb + h0 + nh].rearrange("h (m r) p -> m h r p", r=R)[:, :, r0:r1, :],
+                in_=o_sb[n][hb][:].rearrange("q (h r p) -> q h r p", h=4, r=R)[:, h0:h0 + nh, r0:r1, :],
+            )
+
+        tw("A", 0)
+        tw("A", 1)
+        tw("A", 2)
+        tw("A", 3)
+        cw("A", 0, "s")
+        cw("A", 1, "v")
+        cw("A", 2, "s")
+        cw("A", 3, "v")
+        tx(0, 0)
+        tx(0, 1)
+        qw("A", 0, 2048)
+        cx(0, 0, "s")
+        cx(0, 1, "v")
+        qw("A", 2048, 4096)
+        tx(0, 2)
+        tx(0, 3)
+        qx(0, 0, 2048)
+        cx(0, 2, "s")
+        cx(0, 3, "v")
+        tw("E", 0)
+        cw("E", 0, "s")
+        tx(1, 0)
+        tx(1, 1)
+        qx(0, 2048, 4096)
+        sh(0, 3)
+        qw("E", 0, 1024)
+        qs(0, 1024, 2048)
+        mx(0, 0, 0, 0, 0, "A", 0, 512, 0, True, False)
+        mx(0, 0, 1, 0, 0, "A", 0, 512, 0, True, False)
+        mx(0, 0, 2, 0, 0, "A", 0, 512, 0, True, False)
+        mx(0, 0, 3, 0, 0, "A", 0, 512, 0, True, False)
+        cx(1, 0, "s")
+        cx(1, 1, "s")
+        tx(1, 2)
+        tx(1, 3)
+        cx(1, 2, "s")
+        cx(1, 3, "s")
+        mx(0, 0, 1, 1, 0, "E", 0, 128, 384, False, False)
+        mx(0, 0, 1, 1, 1, "E", 128, 128, 384, False, False)
+        mx(0, 0, 1, 0, 1, "A", 512, 512, 0, False, True)
+        mx(0, 0, 2, 1, 0, "E", 0, 128, 384, False, False)
+        mx(0, 0, 2, 1, 1, "E", 128, 128, 384, False, False)
+        mx(0, 0, 2, 0, 1, "A", 512, 512, 0, False, True)
+        mx(0, 0, 3, 1, 0, "E", 0, 128, 384, False, False)
+        mx(0, 0, 3, 1, 1, "E", 128, 128, 384, False, False)
+        mx(0, 0, 3, 0, 1, "A", 512, 512, 0, False, True)
+        mx(0, 0, 0, 1, 0, "E", 0, 128, 384, False, False)
+        mx(0, 0, 0, 1, 1, "E", 128, 128, 384, False, False)
+        mx(0, 0, 0, 0, 1, "A", 512, 512, 0, False, True)
+        qx(1, 0, 2048)
+        ev(0, 0, 1)
+        qx(1, 2048, 4096)
+        sh(1, 3)
+        qs(1, 1024, 2048)
+        ev(0, 0, 2)
+        ev(0, 0, 3)
+        ev(0, 0, 0)
+        st(0, 0, 0, 4)
+        tw("B", 0)
+        tw("B", 1)
+        tw("B", 2)
+        tw("B", 3)
+        cw("B", 0, "s")
+        cw("B", 1, "s")
+        cw("B", 2, "s")
+        cw("B", 3, "s")
+        mx(1, 0, 0, 0, 0, "A", 0, 512, 0, True, False)
+        mx(1, 0, 1, 0, 0, "A", 0, 512, 0, True, False)
+        mx(1, 0, 2, 0, 0, "A", 0, 512, 0, True, False)
+        mx(1, 0, 3, 0, 0, "A", 0, 512, 0, True, False)
+        mx(1, 0, 1, 1, 0, "E", 0, 128, 384, False, False)
+        mx(1, 0, 1, 1, 1, "E", 128, 128, 384, False, False)
+        mx(1, 0, 1, 0, 1, "A", 512, 512, 0, False, True)
+        mx(1, 0, 2, 1, 0, "E", 0, 128, 384, False, False)
+        mx(1, 0, 2, 1, 1, "E", 128, 128, 384, False, False)
+        mx(1, 0, 2, 0, 1, "A", 512, 512, 0, False, True)
+        mx(1, 0, 3, 1, 0, "E", 0, 128, 384, False, False)
+        mx(1, 0, 3, 1, 1, "E", 128, 128, 384, False, False)
+        mx(1, 0, 3, 0, 1, "A", 512, 512, 0, False, True)
+        mx(1, 0, 0, 1, 0, "E", 0, 128, 384, False, False)
+        mx(1, 0, 0, 1, 1, "E", 128, 128, 384, False, False)
+        mx(1, 0, 0, 0, 1, "A", 512, 512, 0, False, True)
+        qw("B", 0, 2048)
+        qw("B", 2048, 4096)
+        ev(1, 0, 1)
+        ev(1, 0, 2)
+        ev(1, 0, 3)
+        ev(1, 0, 0)
+        st(1, 0, 0, 4)
+        tw("C", 0)
+        tw("C", 1)
+        tw("C", 2)
+        tw("C", 3)
+        cw("C", 0, "s")
+        cw("C", 1, "s")
+        cw("C", 2, "s")
+        cw("C", 3, "s")
+        tw("F", 0)
+        tw("F", 1)
+        tw("F", 2)
+        cw("F", 0, "s")
+        cw("F", 1, "s")
+        cw("F", 2, "s")
+        sh(0, 2)
+        qs(0, 0, 1024)
+        mx(0, 1, 0, 0, 0, "B", 0, 512, 0, True, False)
+        mx(0, 1, 0, 0, 1, "B", 512, 512, 0, False, False)
+        mx(0, 1, 1, 0, 0, "B", 0, 512, 0, True, False)
+        mx(0, 1, 1, 0, 1, "B", 512, 512, 0, False, False)
+        mx(0, 1, 2, 0, 0, "B", 0, 512, 0, True, False)
+        mx(0, 1, 2, 0, 1, "B", 512, 512, 0, False, False)
+        mx(0, 1, 3, 0, 0, "B", 0, 512, 0, True, False)
+        mx(0, 1, 3, 0, 1, "B", 512, 512, 0, False, False)
+        qw("C", 0, 2048)
+        qw("C", 2048, 4096)
+        mx(0, 1, 0, 1, 0, "C", 0, 512, 0, False, False)
+        mx(0, 1, 1, 1, 0, "C", 0, 512, 0, False, False)
+        mx(0, 1, 2, 1, 0, "C", 0, 512, 0, False, False)
+        mx(0, 1, 3, 1, 0, "C", 0, 512, 0, False, False)
+        qw("F", 0, 2048)
+        qw("F", 2048, 3072)
+        sh(1, 2)
+        qs(1, 0, 1024)
+        mx(0, 1, 0, 2, 0, "F", 0, 128, 128, False, False)
+        mx(0, 1, 0, 2, 0, "F", 128, 256, 256, False, False)
+        mx(0, 1, 0, 2, 1, "F", 384, 128, 128, False, False)
+        mx(0, 1, 0, 2, 1, "F", 512, 256, 256, False, False)
+        mx(0, 1, 0, 1, 1, "C", 512, 512, 0, False, True)
+        ev(0, 1, 0)
+        mx(0, 1, 1, 2, 0, "F", 0, 128, 128, False, False)
+        mx(0, 1, 1, 2, 0, "F", 128, 256, 256, False, False)
+        mx(0, 1, 1, 2, 1, "F", 384, 128, 128, False, False)
+        mx(0, 1, 1, 2, 1, "F", 512, 256, 256, False, False)
+        mx(0, 1, 1, 1, 1, "C", 512, 512, 0, False, True)
+        ev(0, 1, 1)
+        mx(0, 1, 2, 2, 0, "F", 0, 128, 128, False, False)
+        mx(0, 1, 2, 2, 0, "F", 128, 256, 256, False, False)
+        mx(0, 1, 2, 2, 1, "F", 384, 128, 128, False, False)
+        mx(0, 1, 2, 2, 1, "F", 512, 256, 256, False, False)
+        mx(0, 1, 2, 1, 1, "C", 512, 512, 0, False, True)
+        ev(0, 1, 2)
+        mx(0, 1, 3, 2, 0, "F", 0, 128, 128, False, False)
+        mx(0, 1, 3, 2, 0, "F", 128, 256, 256, False, False)
+        mx(0, 1, 3, 2, 1, "F", 384, 128, 128, False, False)
+        mx(0, 1, 3, 2, 1, "F", 512, 256, 256, False, False)
+        mx(0, 1, 3, 1, 1, "C", 512, 512, 0, False, True)
+        ev(0, 1, 3)
+        st(0, 1, 0, 4)
+        mx(1, 1, 0, 0, 0, "B", 0, 512, 0, True, False)
+        mx(1, 1, 0, 2, 0, "F", 0, 128, 128, False, False)
+        mx(1, 1, 0, 2, 0, "F", 128, 256, 256, False, False)
+        mx(1, 1, 0, 1, 0, "C", 0, 512, 0, False, False)
+        mx(1, 1, 0, 0, 1, "B", 512, 512, 0, False, False)
+        mx(1, 1, 0, 2, 1, "F", 384, 128, 128, False, False)
+        mx(1, 1, 0, 2, 1, "F", 512, 256, 256, False, False)
+        mx(1, 1, 0, 1, 1, "C", 512, 512, 0, False, True)
+        ev(1, 1, 0)
+        mx(1, 1, 1, 0, 0, "B", 0, 512, 0, True, False)
+        mx(1, 1, 1, 2, 0, "F", 0, 128, 128, False, False)
+        mx(1, 1, 1, 2, 0, "F", 128, 256, 256, False, False)
+        mx(1, 1, 1, 1, 0, "C", 0, 512, 0, False, False)
+        mx(1, 1, 1, 0, 1, "B", 512, 512, 0, False, False)
+        mx(1, 1, 1, 2, 1, "F", 384, 128, 128, False, False)
+        mx(1, 1, 1, 2, 1, "F", 512, 256, 256, False, False)
+        mx(1, 1, 1, 1, 1, "C", 512, 512, 0, False, True)
+        ev(1, 1, 1)
+        st(1, 1, 0, 2)
+        mx(1, 1, 2, 0, 0, "B", 0, 512, 0, True, False)
+        mx(1, 1, 2, 2, 0, "F", 0, 128, 128, False, False)
+        mx(1, 1, 2, 2, 0, "F", 128, 256, 256, False, False)
+        mx(1, 1, 2, 1, 0, "C", 0, 512, 0, False, False)
+        mx(1, 1, 2, 0, 1, "B", 512, 512, 0, False, False)
+        mx(1, 1, 2, 2, 1, "F", 384, 128, 128, False, False)
+        mx(1, 1, 2, 2, 1, "F", 512, 256, 256, False, False)
+        mx(1, 1, 2, 1, 1, "C", 512, 512, 0, False, True)
+        ev(1, 1, 2)
+        st(1, 1, 2, 3)
+        mx(1, 2, 3, 0, 0, "B", 0, 256, 0, True, False)
+        mx(1, 2, 3, 2, 0, "F", 0, 128, 128, False, False)
+        mx(1, 2, 3, 1, 0, "C", 0, 256, 0, False, False)
+        mx(1, 2, 3, 0, 1, "B", 512, 256, 0, False, False)
+        mx(1, 2, 3, 2, 1, "F", 384, 128, 128, False, False)
+        mx(1, 2, 3, 1, 1, "C", 512, 256, 0, False, True)
+        ev(1, 2, 3)
+        st(1, 2, 3, 4)
+        mx(1, 3, 3, 0, 0, "B", 256, 256, 256, True, False)
+        mx(1, 3, 3, 2, 0, "F", 128, 256, 256, False, False)
+        mx(1, 3, 3, 1, 0, "C", 256, 256, 256, False, False)
+        mx(1, 3, 3, 0, 1, "B", 768, 256, 256, False, False)
+        mx(1, 3, 3, 2, 1, "F", 512, 256, 256, False, False)
+        mx(1, 3, 3, 1, 1, "C", 768, 256, 256, False, True)
+        ev(1, 3, 3)
+        st(1, 3, 3, 4)

@@ -13,6 +13,7 @@ ADD = mybir.AluOpType.add
 B, S, D, P, H = 2, 512, 1024, 128, 8
 R = 4
 G = 2
+W = D // 2
 FLOPS = 2 * B * S * D * P * 16
 
 
@@ -21,6 +22,7 @@ def tile_multiheadhomogeneousattention_pa_kernel(tc, x, w_now, w_back1, w_back2,
     with ExitStack() as ctx:
         const = ctx.enter_context(tc.tile_pool(name="const", bufs=1))
         raw = ctx.enter_context(tc.tile_pool(name="raw", bufs=1))
+        srt = ctx.enter_context(tc.tile_pool(name="srt", bufs=1))
         grp = ctx.enter_context(tc.tile_pool(name="grp", bufs=1))
         mxp = ctx.enter_context(tc.tile_pool(name="mxp", bufs=1))
         outp = ctx.enter_context(tc.tile_pool(name="outp", bufs=1))
@@ -33,21 +35,16 @@ def tile_multiheadhomogeneousattention_pa_kernel(tc, x, w_now, w_back1, w_back2,
         bias_row = const.tile([P, H * P], BF16, name="bias_row")
         bias_all = const.tile([P, H * P], F32, name="bias_all")
         heads = {"A": 4, "B": 4, "C": 4, "E": 1, "F": 3}
-        w_raw, w_grp, w_code, w_scale = {}, {}, {}, {}
-        for k in ("A", "E", "B", "C", "F"):
-            nh = heads[k]
-            w_raw[k] = raw.tile([P, nh * D], BF16, name="w_raw" + k)
-            w_grp[k] = grp.tile([P, nh * D], BF16, name="w_grp" + k, align_bytes=64)
-            w_code[k] = mxp.tile([P, nh * D // 4], U32, name="w_code" + k, align_bytes=64)
-            w_scale[k] = mxp.tile([P, nh * D // 4], U8, name="w_scale" + k, align_bytes=64)
-        x_raw, x_grp, x_code, x_scale = [], [], [], []
+        t_raw, t_srt, t_grp, t_code, t_scale = {}, {}, {}, {}, {}
+        for k in ("A", "E", "B", "C", "F", 0, 1):
+            nh = heads.get(k, R)
+            t_raw[k] = raw.tile([P, nh * D], BF16, name="raw_%s" % k)
+            t_grp[k] = grp.tile([P, nh * D], BF16, name="grp_%s" % k, align_bytes=64)
+            t_code[k] = mxp.tile([P, nh * D // 4], U32, name="code_%s" % k, align_bytes=64)
+            t_scale[k] = mxp.tile([P, nh * D // 4], U8, name="scale_%s" % k, align_bytes=64)
         s_grp, s_code, s_scale = [], [], []
         o_sb = []
         for n in range(B):
-            x_raw.append(raw.tile([P, R * D], BF16, name="x_raw%d" % n))
-            x_grp.append(grp.tile([P, R * D], BF16, name="x_grp%d" % n, align_bytes=64))
-            x_code.append(mxp.tile([P, R * D // 4], U32, name="x_code%d" % n, align_bytes=64))
-            x_scale.append(mxp.tile([P, R * D // 4], U8, name="x_scale%d" % n, align_bytes=64))
             s_grp.append(grp.tile([P, 2 * D], BF16, name="s_grp%d" % n, align_bytes=64))
             s_code.append(mxp.tile([P, 2 * D // 4], U32, name="s_code%d" % n, align_bytes=64))
             s_scale.append(mxp.tile([P, 2 * D // 4], U8, name="s_scale%d" % n, align_bytes=64))
@@ -55,21 +52,24 @@ def tile_multiheadhomogeneousattention_pa_kernel(tc, x, w_now, w_back1, w_back2,
 
         def load_w(k, src, h0, h1):
             nc.sync.dma_start(
-                out=w_raw[k][:, h0 * D:h1 * D].rearrange("p (h d) -> p h d", h=h1 - h0),
+                out=t_raw[k][:, h0 * D:h1 * D].rearrange("p (h d) -> p h d", h=h1 - h0),
                 in_=src.rearrange("h p d -> p h d"),
             )
 
         def load_x(n, r0, r1):
             nc.sync.dma_start(
-                out=x_raw[n][:, r0 * D:r1 * D],
+                out=t_raw[n][:, r0 * D:r1 * D],
                 in_=x[n].rearrange("(m r) d -> m (r d)", r=R)[:, r0 * D:r1 * D],
             )
 
-        nc.sync.dma_start(out=bias_in[:], in_=bias.rearrange("(o h) p -> o (h p)", o=1))
-        load_w("A", w_now[0:2], 0, 2)
-        load_w("A", w_now[2:4], 2, 4)
-        load_x(0, 0, 2)
+        load_w("A", w_now[0:1], 0, 1)
+        load_w("A", w_now[1:2], 1, 2)
+        load_w("A", w_now[2:3], 2, 3)
+        load_w("A", w_now[3:4], 3, 4)
+        load_x(0, 0, 1)
+        load_x(0, 1, 2)
         load_x(0, 2, 4)
+        nc.sync.dma_start(out=bias_in[:], in_=bias.rearrange("(o h) p -> o (h p)", o=1))
         load_w("E", w_back1[0:1], 0, 1)
         load_x(1, 0, 2)
         load_x(1, 2, 4)
@@ -83,12 +83,8 @@ def tile_multiheadhomogeneousattention_pa_kernel(tc, x, w_now, w_back1, w_back2,
         nc.vector.memset(ones[:], 1.0)
         nc.vector.memset(bias_row[:], 0.0)
         for n in range(B):
-            nc.vector.memset(s_grp[n][:].bitcast(F32), 0.0)
-        nc.vector.tensor_copy(out=bias_row[0:1, :], in_=bias_in[:])
-        for hf in range(2):
-            bb = psum.tile([P, 512], F32, name="bb", tag="bank")
-            nc.tensor.matmul(bb[:], lhsT=ones[:], rhs=bias_row[:, hf * 512:(hf + 1) * 512], start=True, stop=True)
-            nc.scalar.copy(out=bias_all[:, hf * 512:(hf + 1) * 512], in_=bb[:])
+            first = s_grp[n][:].rearrange("q (t g c) -> q t g c", t=2, g=G)[:, :, :, 0:4]
+            nc.vector.memset(first, 0.0)
 
         flipped = {}
         accs = {}
@@ -99,12 +95,44 @@ def tile_multiheadhomogeneousattention_pa_kernel(tc, x, w_now, w_back1, w_back2,
             else:
                 nc.scalar.copy(out=dst, in_=src)
 
-        def flip(words):
+        def spread_bias():
+            for hf in range(2):
+                bb = psum.tile([P, 512], F32, name="bb", tag="bank")
+                nc.tensor.matmul(bb[:], lhsT=ones[:], rhs=bias_row[:, hf * 512:(hf + 1) * 512], start=True, stop=True)
+                nc.scalar.copy(out=bias_all[:, hf * 512:(hf + 1) * 512], in_=bb[:])
+
+        def so(k, j, eng):
+            t_srt[(k, j)] = srt.tile([P, W], F32, name="srt_%s_%d" % (k, j))
+            copy_on(
+                eng,
+                t_srt[(k, j)][:].rearrange("p (g u q) -> p g u q", g=G, u=2),
+                t_raw[k][:].bitcast(F32)[:, j * W:(j + 1) * W].rearrange("p (g q u) -> p g u q", g=G, u=2),
+            )
+
+        def tr(k, j):
             bank = psum.tile([P, 512], F32, name="bank", tag="bank")
             for c in range(4):
                 g, u = divmod(c, 2)
-                nc.tensor.transpose(bank[:, c * P:(c + 1) * P], words[:, g * 256 + u:(g + 1) * 256:2], ident[:])
-            return bank[:].rearrange("q (g u m) -> q g m u", g=G, u=2)
+                if (k, j) in t_srt:
+                    words = t_srt[(k, j)][:, c * P:(c + 1) * P]
+                else:
+                    words = t_raw[k][:].bitcast(F32)[:, j * W + g * 256 + u:j * W + (g + 1) * 256:2]
+                nc.tensor.transpose(bank[:, c * P:(c + 1) * P], words, ident[:])
+            flipped[(k, j)] = bank[:].rearrange("q (g u m) -> q g m u", g=G, u=2)
+
+        def cp(k, j, eng):
+            words = t_grp[k][:].bitcast(F32)
+            if k in heads:
+                dst = words.rearrange("q (g h m u) -> q g h m u", g=G, h=heads[k], u=2)[:, :, j, :, :]
+            else:
+                dst = words[:, j * W:(j + 1) * W].rearrange("q (g m u) -> q g m u", g=G, u=2)
+            copy_on(eng, dst, flipped[(k, j)])
+
+        def sh(n, r):
+            nc.vector.tensor_copy(
+                out=s_grp[n][:].rearrange("q (t g c) -> q t g c", t=2, g=G)[:, r - 2, :, 4:512],
+                in_=t_grp[n][:].rearrange("q (t g c) -> q t g c", t=R, g=G)[:, r, :, 0:508],
+            )
 
         def quant(src, code, scale, c0, c1):
             nc.vector.quantize_mx(
@@ -113,31 +141,13 @@ def tile_multiheadhomogeneousattention_pa_kernel(tc, x, w_now, w_back1, w_back2,
                 in_=src[:, c0:c1],
             )
 
-        def tw(k, h):
-            flipped[(k, h)] = flip(w_raw[k][:].bitcast(F32)[:, h * 512:(h + 1) * 512])
+        def q(k, c0, c1):
+            quant(t_grp[k], t_code[k], t_scale[k], c0, c1)
 
-        def cw(k, h, eng):
-            dst = w_grp[k][:].bitcast(F32).rearrange("q (g h m u) -> q g h m u", g=G, h=heads[k], u=2)
-            copy_on(eng, dst[:, :, h, :, :], flipped[(k, h)])
-
-        def tx(n, r):
-            flipped[(n, r)] = flip(x_raw[n][:].bitcast(F32)[:, r * 512:(r + 1) * 512])
-
-        def cx(n, r, eng):
-            dst = x_grp[n][:].bitcast(F32)[:, r * 512:(r + 1) * 512].rearrange("q (g m u) -> q g m u", g=G, u=2)
-            copy_on(eng, dst, flipped[(n, r)])
-
-        def sh(n, r):
-            nc.vector.tensor_copy(
-                out=s_grp[n][:].rearrange("q (t g c) -> q t g c", t=2, g=G)[:, r - 2, :, 4:512],
-                in_=x_grp[n][:].rearrange("q (t g c) -> q t g c", t=R, g=G)[:, r, :, 0:508],
-            )
-
-        def qw(k, c0, c1):
-            quant(w_grp[k], w_code[k], w_scale[k], c0, c1)
-
-        def qx(n, c0, c1):
-            quant(x_grp[n], x_code[n], x_scale[n], c0, c1)
+        def qh(k, h):
+            for g in range(G):
+                c0 = (g * heads[k] + h) * 512
+                q(k, c0, c0 + 512)
 
         def qs(n, c0, c1):
             quant(s_grp[n], s_code[n], s_scale[n], c0, c1)
@@ -146,7 +156,7 @@ def tile_multiheadhomogeneousattention_pa_kernel(tc, x, w_now, w_back1, w_back2,
             rr = r - j
             if rr >= 0:
                 c = (rr * G + g) * P
-                return x_code[n][:, c:c + P].bitcast(FP8X4), x_scale[n][:, c:c + P]
+                return t_code[n][:, c:c + P].bitcast(FP8X4), t_scale[n][:, c:c + P]
             c = ((rr + 2) * G + g) * P
             return s_code[n][:, c:c + P].bitcast(FP8X4), s_scale[n][:, c:c + P]
 
@@ -158,8 +168,8 @@ def tile_multiheadhomogeneousattention_pa_kernel(tc, x, w_now, w_back1, w_back2,
                 out=accs[(n, hf, r)][:, o0:o0 + width],
                 lhsT=lt,
                 lhsT_scale=ls,
-                rhs=w_code[k][:, c0:c0 + width].bitcast(FP8X4),
-                rhs_scale=w_scale[k][:, c0:c0 + width],
+                rhs=t_code[k][:, c0:c0 + width].bitcast(FP8X4),
+                rhs_scale=t_scale[k][:, c0:c0 + width],
                 start=start,
                 stop=stop,
             )
@@ -182,196 +192,142 @@ def tile_multiheadhomogeneousattention_pa_kernel(tc, x, w_now, w_back1, w_back2,
                 in_=o_sb[n][hb][:].rearrange("q (h r p) -> q h r p", h=4, r=R)[:, h0:h0 + nh, r0:r1, :],
             )
 
-        tw("A", 0)
-        tw("A", 1)
-        tw("A", 2)
-        tw("A", 3)
-        cw("A", 0, "s")
-        cw("A", 1, "v")
-        cw("A", 2, "s")
-        cw("A", 3, "v")
-        tx(0, 0)
-        tx(0, 1)
-        qw("A", 0, 2048)
-        cx(0, 0, "s")
-        cx(0, 1, "v")
-        qw("A", 2048, 4096)
-        tx(0, 2)
-        tx(0, 3)
-        qx(0, 0, 2048)
-        cx(0, 2, "s")
-        cx(0, 3, "v")
-        tw("E", 0)
-        cw("E", 0, "s")
-        tx(1, 0)
-        tx(1, 1)
-        qx(0, 2048, 4096)
+        def a0(n, r):
+            mx(n, 0, r, 0, 0, "A", 0, 512, 0, True, False)
+            mx(n, 0, r, 0, 1, "A", 512, 512, 0, False, False)
+
+        def a1(n, r):
+            mx(n, 0, r, 1, 0, "E", 0, 128, 384, False, False)
+            mx(n, 0, r, 1, 1, "E", 128, 128, 384, False, True)
+
+        def b0(n, r):
+            mx(n, 1, r, 0, 0, "B", 0, 512, 0, True, False)
+            mx(n, 1, r, 0, 1, "B", 512, 512, 0, False, False)
+
+        def b1(n, r, stop):
+            mx(n, 1, r, 1, 0, "C", 0, 512, 0, False, False)
+            mx(n, 1, r, 1, 1, "C", 512, 512, 0, False, stop)
+
+        def b2(n, r):
+            mx(n, 1, r, 2, 0, "F", 0, 128, 128, False, False)
+            mx(n, 1, r, 2, 0, "F", 128, 256, 256, False, False)
+            mx(n, 1, r, 2, 1, "F", 384, 128, 128, False, False)
+            mx(n, 1, r, 2, 1, "F", 512, 256, 256, False, False)
+
+        def b2c(n, r):
+            mx(n, 1, r, 1, 0, "C", 0, 512, 0, False, False)
+            b2(n, r)
+            mx(n, 1, r, 1, 1, "C", 512, 512, 0, False, True)
+
+
+        for h in range(4):
+            tr("A", h)
+            cp("A", h, "sv"[h % 2])
+            if h >= 1:
+                qh("A", h - 1)
+        for r in range(R):
+            tr(0, r)
+            if r == 3:
+                nc.vector.tensor_copy(out=bias_row[0:1, :], in_=bias_in[:])
+            cp(0, r, "sv"[r % 2])
+            if r == 0:
+                qh("A", 3)
+            else:
+                q(0, (r - 1) * D, r * D)
+        tr("E", 0)
+        cp("E", 0, "s")
+        q(0, 3 * D, 4 * D)
         sh(0, 3)
-        qw("E", 0, 1024)
-        qs(0, 1024, 2048)
-        mx(0, 0, 0, 0, 0, "A", 0, 512, 0, True, False)
-        mx(0, 0, 1, 0, 0, "A", 0, 512, 0, True, False)
-        mx(0, 0, 2, 0, 0, "A", 0, 512, 0, True, False)
-        mx(0, 0, 3, 0, 0, "A", 0, 512, 0, True, False)
-        cx(1, 0, "s")
-        cx(1, 1, "s")
-        tx(1, 2)
-        tx(1, 3)
-        cx(1, 2, "s")
-        cx(1, 3, "s")
-        mx(0, 0, 1, 1, 0, "E", 0, 128, 384, False, False)
-        mx(0, 0, 1, 1, 1, "E", 128, 128, 384, False, False)
-        mx(0, 0, 1, 0, 1, "A", 512, 512, 0, False, True)
-        mx(0, 0, 2, 1, 0, "E", 0, 128, 384, False, False)
-        mx(0, 0, 2, 1, 1, "E", 128, 128, 384, False, False)
-        mx(0, 0, 2, 0, 1, "A", 512, 512, 0, False, True)
-        mx(0, 0, 3, 1, 0, "E", 0, 128, 384, False, False)
-        mx(0, 0, 3, 1, 1, "E", 128, 128, 384, False, False)
-        mx(0, 0, 3, 0, 1, "A", 512, 512, 0, False, True)
-        mx(0, 0, 0, 1, 0, "E", 0, 128, 384, False, False)
-        mx(0, 0, 0, 1, 1, "E", 128, 128, 384, False, False)
-        mx(0, 0, 0, 0, 1, "A", 512, 512, 0, False, True)
-        qx(1, 0, 2048)
+        spread_bias()
+        so(1, 0, "v")
+        q("E", 0, D)
+        qs(0, D, 2 * D)
+        a0(0, 0)
+        a0(0, 1)
+        a1(0, 1)
+        a0(0, 2)
+        a1(0, 2)
+        a0(0, 3)
+        a1(0, 3)
+        a1(0, 0)
+        so(1, 1, "v")
+        so(1, 2, "s")
+        so(1, 3, "s")
+        so("B", 0, "s")
+        so("B", 1, "s")
         ev(0, 0, 1)
-        qx(1, 2048, 4096)
-        sh(1, 3)
-        qs(1, 1024, 2048)
         ev(0, 0, 2)
+        so("B", 2, "v")
         ev(0, 0, 3)
         ev(0, 0, 0)
+        so("B", 3, "v")
         st(0, 0, 0, 4)
-        tw("B", 0)
-        tw("B", 1)
-        tw("B", 2)
-        tw("B", 3)
-        cw("B", 0, "s")
-        cw("B", 1, "s")
-        cw("B", 2, "s")
-        cw("B", 3, "s")
-        mx(1, 0, 0, 0, 0, "A", 0, 512, 0, True, False)
-        mx(1, 0, 1, 0, 0, "A", 0, 512, 0, True, False)
-        mx(1, 0, 2, 0, 0, "A", 0, 512, 0, True, False)
-        mx(1, 0, 3, 0, 0, "A", 0, 512, 0, True, False)
-        mx(1, 0, 1, 1, 0, "E", 0, 128, 384, False, False)
-        mx(1, 0, 1, 1, 1, "E", 128, 128, 384, False, False)
-        mx(1, 0, 1, 0, 1, "A", 512, 512, 0, False, True)
-        mx(1, 0, 2, 1, 0, "E", 0, 128, 384, False, False)
-        mx(1, 0, 2, 1, 1, "E", 128, 128, 384, False, False)
-        mx(1, 0, 2, 0, 1, "A", 512, 512, 0, False, True)
-        mx(1, 0, 3, 1, 0, "E", 0, 128, 384, False, False)
-        mx(1, 0, 3, 1, 1, "E", 128, 128, 384, False, False)
-        mx(1, 0, 3, 0, 1, "A", 512, 512, 0, False, True)
-        mx(1, 0, 0, 1, 0, "E", 0, 128, 384, False, False)
-        mx(1, 0, 0, 1, 1, "E", 128, 128, 384, False, False)
-        mx(1, 0, 0, 0, 1, "A", 512, 512, 0, False, True)
-        qw("B", 0, 2048)
-        qw("B", 2048, 4096)
+        for r in range(R):
+            tr(1, r)
+            cp(1, r, "s")
+            if r >= 1:
+                q(1, (r - 1) * D, r * D)
+        q(1, 3 * D, 4 * D)
+        sh(1, 3)
+        for h in range(4):
+            tr("B", h)
+            cp("B", h, "s")
+            if h == 1:
+                qs(1, D, 2 * D)
+        for r in range(R):
+            a0(1, r)
+            if r >= 1:
+                a1(1, r)
+        a1(1, 0)
+        for h in range(4):
+            so("C", h, "vvvs"[h])
+        for h in range(3):
+            so("F", h, "s")
         ev(1, 0, 1)
         ev(1, 0, 2)
         ev(1, 0, 3)
         ev(1, 0, 0)
         st(1, 0, 0, 4)
-        tw("C", 0)
-        tw("C", 1)
-        tw("C", 2)
-        tw("C", 3)
-        cw("C", 0, "s")
-        cw("C", 1, "s")
-        cw("C", 2, "s")
-        cw("C", 3, "s")
-        tw("F", 0)
-        tw("F", 1)
-        tw("F", 2)
-        cw("F", 0, "s")
-        cw("F", 1, "s")
-        cw("F", 2, "s")
+        for g in range(G):
+            q("B", g * 2048, (g + 1) * 2048)
         sh(0, 2)
-        qs(0, 0, 1024)
-        mx(0, 1, 0, 0, 0, "B", 0, 512, 0, True, False)
-        mx(0, 1, 0, 0, 1, "B", 512, 512, 0, False, False)
-        mx(0, 1, 1, 0, 0, "B", 0, 512, 0, True, False)
-        mx(0, 1, 1, 0, 1, "B", 512, 512, 0, False, False)
-        mx(0, 1, 2, 0, 0, "B", 0, 512, 0, True, False)
-        mx(0, 1, 2, 0, 1, "B", 512, 512, 0, False, False)
-        mx(0, 1, 3, 0, 0, "B", 0, 512, 0, True, False)
-        mx(0, 1, 3, 0, 1, "B", 512, 512, 0, False, False)
-        qw("C", 0, 2048)
-        qw("C", 2048, 4096)
-        mx(0, 1, 0, 1, 0, "C", 0, 512, 0, False, False)
-        mx(0, 1, 1, 1, 0, "C", 0, 512, 0, False, False)
-        mx(0, 1, 2, 1, 0, "C", 0, 512, 0, False, False)
-        mx(0, 1, 3, 1, 0, "C", 0, 512, 0, False, False)
-        qw("F", 0, 2048)
-        qw("F", 2048, 3072)
+        qs(0, 0, D)
+        for h in range(4):
+            tr("C", h)
+            cp("C", h, "sv"[h % 2])
+        for h in range(3):
+            tr("F", h)
+            cp("F", h, "s")
+        for r in range(R):
+            b0(0, r)
+        for g in range(G):
+            q("C", g * 2048, (g + 1) * 2048)
+        for h in range(3):
+            qh("F", h)
         sh(1, 2)
-        qs(1, 0, 1024)
-        mx(0, 1, 0, 2, 0, "F", 0, 128, 128, False, False)
-        mx(0, 1, 0, 2, 0, "F", 128, 256, 256, False, False)
-        mx(0, 1, 0, 2, 1, "F", 384, 128, 128, False, False)
-        mx(0, 1, 0, 2, 1, "F", 512, 256, 256, False, False)
-        mx(0, 1, 0, 1, 1, "C", 512, 512, 0, False, True)
-        ev(0, 1, 0)
-        mx(0, 1, 1, 2, 0, "F", 0, 128, 128, False, False)
-        mx(0, 1, 1, 2, 0, "F", 128, 256, 256, False, False)
-        mx(0, 1, 1, 2, 1, "F", 384, 128, 128, False, False)
-        mx(0, 1, 1, 2, 1, "F", 512, 256, 256, False, False)
-        mx(0, 1, 1, 1, 1, "C", 512, 512, 0, False, True)
-        ev(0, 1, 1)
-        mx(0, 1, 2, 2, 0, "F", 0, 128, 128, False, False)
-        mx(0, 1, 2, 2, 0, "F", 128, 256, 256, False, False)
-        mx(0, 1, 2, 2, 1, "F", 384, 128, 128, False, False)
-        mx(0, 1, 2, 2, 1, "F", 512, 256, 256, False, False)
-        mx(0, 1, 2, 1, 1, "C", 512, 512, 0, False, True)
-        ev(0, 1, 2)
-        mx(0, 1, 3, 2, 0, "F", 0, 128, 128, False, False)
-        mx(0, 1, 3, 2, 0, "F", 128, 256, 256, False, False)
-        mx(0, 1, 3, 2, 1, "F", 384, 128, 128, False, False)
-        mx(0, 1, 3, 2, 1, "F", 512, 256, 256, False, False)
-        mx(0, 1, 3, 1, 1, "C", 512, 512, 0, False, True)
-        ev(0, 1, 3)
-        st(0, 1, 0, 4)
-        mx(1, 1, 0, 0, 0, "B", 0, 512, 0, True, False)
-        mx(1, 1, 0, 2, 0, "F", 0, 128, 128, False, False)
-        mx(1, 1, 0, 2, 0, "F", 128, 256, 256, False, False)
-        mx(1, 1, 0, 1, 0, "C", 0, 512, 0, False, False)
-        mx(1, 1, 0, 0, 1, "B", 512, 512, 0, False, False)
-        mx(1, 1, 0, 2, 1, "F", 384, 128, 128, False, False)
-        mx(1, 1, 0, 2, 1, "F", 512, 256, 256, False, False)
-        mx(1, 1, 0, 1, 1, "C", 512, 512, 0, False, True)
-        ev(1, 1, 0)
-        mx(1, 1, 1, 0, 0, "B", 0, 512, 0, True, False)
-        mx(1, 1, 1, 2, 0, "F", 0, 128, 128, False, False)
-        mx(1, 1, 1, 2, 0, "F", 128, 256, 256, False, False)
-        mx(1, 1, 1, 1, 0, "C", 0, 512, 0, False, False)
-        mx(1, 1, 1, 0, 1, "B", 512, 512, 0, False, False)
-        mx(1, 1, 1, 2, 1, "F", 384, 128, 128, False, False)
-        mx(1, 1, 1, 2, 1, "F", 512, 256, 256, False, False)
-        mx(1, 1, 1, 1, 1, "C", 512, 512, 0, False, True)
-        ev(1, 1, 1)
-        st(1, 1, 0, 2)
-        mx(1, 1, 2, 0, 0, "B", 0, 512, 0, True, False)
-        mx(1, 1, 2, 2, 0, "F", 0, 128, 128, False, False)
-        mx(1, 1, 2, 2, 0, "F", 128, 256, 256, False, False)
-        mx(1, 1, 2, 1, 0, "C", 0, 512, 0, False, False)
-        mx(1, 1, 2, 0, 1, "B", 512, 512, 0, False, False)
-        mx(1, 1, 2, 2, 1, "F", 384, 128, 128, False, False)
-        mx(1, 1, 2, 2, 1, "F", 512, 256, 256, False, False)
-        mx(1, 1, 2, 1, 1, "C", 512, 512, 0, False, True)
-        ev(1, 1, 2)
+        qs(1, 0, D)
+        for r in range(R):
+            mx(0, 1, r, 1, 0, "C", 0, 512, 0, False, False)
+        for r in range(R):
+            b2(0, r)
+            mx(0, 1, r, 1, 1, "C", 512, 512, 0, False, True)
+            ev(0, 1, r)
+            if r % 2:
+                st(0, 1, r - 1, r + 1)
+        for r in range(3):
+            b0(1, r)
+            b2c(1, r)
+            ev(1, 1, r)
+            if r == 1:
+                st(1, 1, 0, 2)
         st(1, 1, 2, 3)
-        mx(1, 2, 3, 0, 0, "B", 0, 256, 0, True, False)
-        mx(1, 2, 3, 2, 0, "F", 0, 128, 128, False, False)
-        mx(1, 2, 3, 1, 0, "C", 0, 256, 0, False, False)
-        mx(1, 2, 3, 0, 1, "B", 512, 256, 0, False, False)
-        mx(1, 2, 3, 2, 1, "F", 384, 128, 128, False, False)
-        mx(1, 2, 3, 1, 1, "C", 512, 256, 0, False, True)
-        ev(1, 2, 3)
-        st(1, 2, 3, 4)
-        mx(1, 3, 3, 0, 0, "B", 256, 256, 256, True, False)
-        mx(1, 3, 3, 2, 0, "F", 128, 256, 256, False, False)
-        mx(1, 3, 3, 1, 0, "C", 256, 256, 256, False, False)
-        mx(1, 3, 3, 0, 1, "B", 768, 256, 256, False, False)
-        mx(1, 3, 3, 2, 1, "F", 512, 256, 256, False, False)
-        mx(1, 3, 3, 1, 1, "C", 768, 256, 256, False, True)
-        ev(1, 3, 3)
-        st(1, 3, 3, 4)
+        for hf, c, width in ((2, 0, 128), (3, 128, 256)):
+            o0 = 256 * (hf - 2)
+            mx(1, hf, 3, 0, 0, "B", o0, 256, o0, True, False)
+            mx(1, hf, 3, 0, 1, "B", 512 + o0, 256, o0, False, False)
+            mx(1, hf, 3, 1, 0, "C", o0, 256, o0, False, False)
+            mx(1, hf, 3, 2, 0, "F", c, width, 512 - 3 * 128 + c, False, False)
+            mx(1, hf, 3, 2, 1, "F", 384 + c, width, 512 - 3 * 128 + c, False, False)
+            mx(1, hf, 3, 1, 1, "C", 512 + o0, 256, o0, False, True)
+            ev(1, hf, 3)
+            st(1, hf, 3, 4)

@@ -31,6 +31,7 @@ def tile_multiheadhomogeneousattention_pa_kernel(tc, x, w_now, w_back1, w_back2,
 
         ident = const.tile([P, P], F32, name="ident")
         ones = const.tile([P, P], BF16, name="ones")
+        warm = const.tile([P, 512], BF16, name="warm")
         bias_in = const.tile([1, H * P], BF16, name="bias_in")
         bias_row = const.tile([P, H * P], BF16, name="bias_row")
         bias_all = const.tile([P, H * P], F32, name="bias_all")
@@ -80,6 +81,7 @@ def tile_multiheadhomogeneousattention_pa_kernel(tc, x, w_now, w_back1, w_back2,
         load_w("F", w_back2[0:3], 0, 3)
 
         make_identity(nc, ident[:])
+        nc.vector.memset(warm[:], 0.0)
         nc.vector.memset(ones[:], 1.0)
         nc.vector.memset(bias_row[:], 0.0)
         for n in range(B):
@@ -109,8 +111,10 @@ def tile_multiheadhomogeneousattention_pa_kernel(tc, x, w_now, w_back1, w_back2,
                 t_raw[k][:].bitcast(F32)[:, j * W:(j + 1) * W].rearrange("p (g q u) -> p g u q", g=G, u=2),
             )
 
-        def tr(k, j):
+        def tr(k, j, dummies=0):
             bank = psum.tile([P, 512], F32, name="bank", tag="bank")
+            for i in range(dummies):
+                nc.tensor.matmul(bank[:], lhsT=warm[:, 0:P], rhs=warm[:], start=True, stop=True)
             for c in range(4):
                 g, u = divmod(c, 2)
                 if (k, j) in t_srt:
@@ -144,13 +148,8 @@ def tile_multiheadhomogeneousattention_pa_kernel(tc, x, w_now, w_back1, w_back2,
         def q(k, c0, c1):
             quant(t_grp[k], t_code[k], t_scale[k], c0, c1)
 
-        def qh(k, h):
-            for g in range(G):
-                c0 = (g * heads[k] + h) * 512
-                q(k, c0, c0 + 512)
-
-        def qs(n, c0, c1):
-            quant(s_grp[n], s_code[n], s_scale[n], c0, c1)
+        def qs(n, t):
+            quant(s_grp[n], s_code[n], s_scale[n], t * D, (t + 1) * D)
 
         def stat(n, r, j, g):
             rr = r - j
@@ -223,78 +222,63 @@ def tile_multiheadhomogeneousattention_pa_kernel(tc, x, w_now, w_back1, w_back2,
         for h in range(4):
             tr("A", h)
             cp("A", h, "sv"[h % 2])
-            if h >= 1:
-                qh("A", h - 1)
-        for r in range(R):
-            tr(0, r)
-            if r == 3:
-                nc.vector.tensor_copy(out=bias_row[0:1, :], in_=bias_in[:])
-            cp(0, r, "sv"[r % 2])
-            if r == 0:
-                qh("A", 3)
-            else:
-                q(0, (r - 1) * D, r * D)
+        tr(0, 0)
+        cp(0, 0, "s")
+        q("A", 0, 2048)
+        tr(0, 1)
+        cp(0, 1, "s")
+        q(0, 0, 1024)
+        q("A", 2048, 4096)
+        nc.vector.tensor_copy(out=bias_row[0:1, :], in_=bias_in[:])
+        tr(0, 2)
+        cp(0, 2, "s")
+        q(0, 1024, 2048)
+        tr(0, 3)
+        cp(0, 3, "v")
         tr("E", 0)
         cp("E", 0, "s")
-        q(0, 3 * D, 4 * D)
-        sh(0, 3)
         spread_bias()
-        so(1, 0, "v")
+        q(0, 2048, 4096)
+        sh(0, 3)
         q("E", 0, D)
-        qs(0, D, 2 * D)
-        a0(0, 0)
-        a0(0, 1)
-        a1(0, 1)
-        a0(0, 2)
-        a1(0, 2)
-        a0(0, 3)
-        a1(0, 3)
+        qs(0, 1)
+        for r in range(R):
+            a0(0, r)
+            if r >= 1:
+                a1(0, r)
         a1(0, 0)
-        so(1, 1, "v")
-        so(1, 2, "s")
-        so(1, 3, "s")
-        so("B", 0, "s")
-        so("B", 1, "s")
         ev(0, 0, 1)
         ev(0, 0, 2)
-        so("B", 2, "v")
         ev(0, 0, 3)
         ev(0, 0, 0)
-        so("B", 3, "v")
         st(0, 0, 0, 4)
         for r in range(R):
             tr(1, r)
             cp(1, r, "s")
-            if r >= 1:
-                q(1, (r - 1) * D, r * D)
-        q(1, 3 * D, 4 * D)
+        q(1, 0, 2048)
+        q(1, 2048, 4096)
         sh(1, 3)
         for h in range(4):
             tr("B", h)
             cp("B", h, "s")
-            if h == 1:
-                qs(1, D, 2 * D)
+        qs(1, 1)
         for r in range(R):
             a0(1, r)
             if r >= 1:
                 a1(1, r)
         a1(1, 0)
-        for h in range(4):
-            so("C", h, "vvvs"[h])
-        for h in range(3):
-            so("F", h, "s")
+        for g in range(G):
+            q("B", g * 2048, (g + 1) * 2048)
         ev(1, 0, 1)
         ev(1, 0, 2)
         ev(1, 0, 3)
         ev(1, 0, 0)
         st(1, 0, 0, 4)
-        for g in range(G):
-            q("B", g * 2048, (g + 1) * 2048)
         sh(0, 2)
-        qs(0, 0, D)
+        qs(0, 0)
         for h in range(4):
             tr("C", h)
-            cp("C", h, "sv"[h % 2])
+            cp("C", h, "s")
         for h in range(3):
             tr("F", h)
             cp("F", h, "s")
@@ -302,10 +286,10 @@ def tile_multiheadhomogeneousattention_pa_kernel(tc, x, w_now, w_back1, w_back2,
             b0(0, r)
         for g in range(G):
             q("C", g * 2048, (g + 1) * 2048)
-        for h in range(3):
-            qh("F", h)
         sh(1, 2)
-        qs(1, 0, D)
+        qs(1, 0)
+        q("F", 0, 2048)
+        q("F", 2048, 3072)
         for r in range(R):
             mx(0, 1, r, 1, 0, "C", 0, 512, 0, False, False)
         for r in range(R):

@@ -103,12 +103,15 @@ def tile_multiheadhomogeneousattention_pa_kernel(tc, x, w_now, w_back1, w_back2,
                 nc.tensor.matmul(bb[:], lhsT=ones[:], rhs=bias_row[:, hf * 512:(hf + 1) * 512], start=True, stop=True)
                 nc.scalar.copy(out=bias_all[:, hf * 512:(hf + 1) * 512], in_=bb[:])
 
-        def so(k, j, eng):
-            t_srt[(k, j)] = srt.tile([P, W], F32, name="srt_%s_%d" % (k, j))
+        def so(k, j0, j1, eng):
+            nj = j1 - j0
+            tile = srt.tile([P, nj * W], F32, name="srt_%s_%d" % (k, j0))
+            for j in range(j0, j1):
+                t_srt[(k, j)] = tile[:, (j - j0) * W:(j - j0 + 1) * W]
             copy_on(
                 eng,
-                t_srt[(k, j)][:].rearrange("p (g u q) -> p g u q", g=G, u=2),
-                t_raw[k][:].bitcast(F32)[:, j * W:(j + 1) * W].rearrange("p (g q u) -> p g u q", g=G, u=2),
+                tile[:].rearrange("p (g u q) -> p g u q", g=nj * G, u=2),
+                t_raw[k][:].bitcast(F32)[:, j0 * W:j1 * W].rearrange("p (g q u) -> p g u q", g=nj * G, u=2),
             )
 
         def tr(k, j, dummies=0):
@@ -247,8 +250,10 @@ def tile_multiheadhomogeneousattention_pa_kernel(tc, x, w_now, w_back1, w_back2,
             if r >= 1:
                 a1(0, r)
         a1(0, 0)
+        so("B", 0, 2, "s")
         ev(0, 0, 1)
         ev(0, 0, 2)
+        so("B", 2, 4, "v")
         ev(0, 0, 3)
         ev(0, 0, 0)
         st(0, 0, 0, 4)
@@ -269,6 +274,9 @@ def tile_multiheadhomogeneousattention_pa_kernel(tc, x, w_now, w_back1, w_back2,
         a1(1, 0)
         for g in range(G):
             q("B", g * 2048, (g + 1) * 2048)
+        so("C", 2, 4, "v")
+        so("C", 0, 2, "s")
+        so("F", 0, 3, "s")
         ev(1, 0, 1)
         ev(1, 0, 2)
         ev(1, 0, 3)

@@ -26,7 +26,7 @@ def tile_multiheadhomogeneousattention_pa_kernel(tc, x, w_now, w_back1, w_back2,
         grp = ctx.enter_context(tc.tile_pool(name="grp", bufs=1))
         mxp = ctx.enter_context(tc.tile_pool(name="mxp", bufs=1))
         outp = ctx.enter_context(tc.tile_pool(name="outp", bufs=1))
-        psum = ctx.enter_context(tc.psum_pool(name="psum", bufs=8))
+        psum = ctx.enter_context(tc.psum_pool(name="psum", bufs=4))
         ctx.enter_context(tc.manual_schedule())
 
         ident = const.tile([P, P], F32, name="ident")
@@ -67,10 +67,10 @@ def tile_multiheadhomogeneousattention_pa_kernel(tc, x, w_now, w_back1, w_back2,
         load_w("A", w_now[1:2], 1, 2)
         load_w("A", w_now[2:3], 2, 3)
         load_w("A", w_now[3:4], 3, 4)
+        nc.sync.dma_start(out=bias_in[:], in_=bias.rearrange("(o h) p -> o (h p)", o=1))
         load_x(0, 0, 1)
         load_x(0, 1, 2)
         load_x(0, 2, 4)
-        nc.sync.dma_start(out=bias_in[:], in_=bias.rearrange("(o h) p -> o (h p)", o=1))
         load_w("E", w_back1[0:1], 0, 1)
         load_x(1, 0, 2)
         load_x(1, 2, 4)
@@ -164,7 +164,7 @@ def tile_multiheadhomogeneousattention_pa_kernel(tc, x, w_now, w_back1, w_back2,
 
         def mx(n, hf, r, j, g, k, c0, width, o0, start, stop):
             if start:
-                accs[(n, hf, r)] = psum.tile([P, 512], F32, name="acc", tag="bank")
+                accs[(n, hf, r)] = psum.tile([P, 512], F32, name="acc", tag="acc")
             lt, ls = stat(n, r, j, g)
             nc.tensor.matmul_mx(
                 out=accs[(n, hf, r)][:, o0:o0 + width],
@@ -210,11 +210,11 @@ def tile_multiheadhomogeneousattention_pa_kernel(tc, x, w_now, w_back1, w_back2,
             mx(n, 1, r, 1, 0, "C", 0, 512, 0, False, False)
             mx(n, 1, r, 1, 1, "C", 512, 512, 0, False, stop)
 
-        def b2(n, r):
+        def b2(n, r, stop=False):
             mx(n, 1, r, 2, 0, "F", 0, 128, 128, False, False)
             mx(n, 1, r, 2, 0, "F", 128, 256, 256, False, False)
             mx(n, 1, r, 2, 1, "F", 384, 128, 128, False, False)
-            mx(n, 1, r, 2, 1, "F", 512, 256, 256, False, False)
+            mx(n, 1, r, 2, 1, "F", 512, 256, 256, False, stop)
 
         def b2c(n, r):
             mx(n, 1, r, 1, 0, "C", 0, 512, 0, False, False)
@@ -222,6 +222,7 @@ def tile_multiheadhomogeneousattention_pa_kernel(tc, x, w_now, w_back1, w_back2,
             mx(n, 1, r, 1, 1, "C", 512, 512, 0, False, True)
 
 
+        order = (1, 2, 3, 0)
         for h in range(4):
             tr("A", h)
             cp("A", h, "sv"[h % 2])
@@ -229,83 +230,70 @@ def tile_multiheadhomogeneousattention_pa_kernel(tc, x, w_now, w_back1, w_back2,
         cp(0, 0, "s")
         q("A", 0, 2048)
         tr(0, 1)
-        cp(0, 1, "s")
-        q(0, 0, 1024)
-        q("A", 2048, 4096)
+        cp(0, 1, "v")
         nc.vector.tensor_copy(out=bias_row[0:1, :], in_=bias_in[:])
+        q("A", 2048, 4096)
         tr(0, 2)
         cp(0, 2, "s")
-        q(0, 1024, 2048)
+        q(0, 0, 2048)
         tr(0, 3)
         cp(0, 3, "v")
         tr("E", 0)
         cp("E", 0, "s")
-        spread_bias()
         q(0, 2048, 4096)
         sh(0, 3)
         q("E", 0, D)
+        spread_bias()
         qs(0, 1)
-        for r in range(R):
-            a0(0, r)
-            if r >= 1:
-                a1(0, r)
-        a1(0, 0)
-        so("B", 0, 2, "s")
-        ev(0, 0, 1)
-        ev(0, 0, 2)
-        so("B", 2, 4, "v")
-        ev(0, 0, 3)
-        ev(0, 0, 0)
-        st(0, 0, 0, 4)
         for r in range(R):
             tr(1, r)
             cp(1, r, "s")
+        so("B", 0, 2, "s")
+        so("B", 2, 4, "s")
         q(1, 0, 2048)
         q(1, 2048, 4096)
         sh(1, 3)
+        qs(1, 1)
+        for r in order:
+            a0(0, r)
+            a1(0, r)
+            ev(0, 0, r)
+        st(0, 0, 0, 4)
         for h in range(4):
             tr("B", h)
             cp("B", h, "s")
-        qs(1, 1)
-        for r in range(R):
-            a0(1, r)
-            if r >= 1:
-                a1(1, r)
-        a1(1, 0)
-        for g in range(G):
-            q("B", g * 2048, (g + 1) * 2048)
-        so("C", 2, 4, "v")
         so("C", 0, 2, "s")
-        so("F", 0, 3, "s")
-        ev(1, 0, 1)
-        ev(1, 0, 2)
-        ev(1, 0, 3)
-        ev(1, 0, 0)
+        so("C", 2, 4, "v")
+        q("B", 0, 2048)
+        q("B", 2048, 4096)
+        for r in order:
+            a0(1, r)
+            a1(1, r)
+            ev(1, 0, r)
         st(1, 0, 0, 4)
-        sh(0, 2)
-        qs(0, 0)
+        so("F", 0, 3, "v")
         for h in range(4):
             tr("C", h)
             cp("C", h, "s")
+        for r in order:
+            b0(0, r)
+        sh(0, 2)
+        qs(0, 0)
         for h in range(3):
             tr("F", h)
             cp("F", h, "s")
-        for r in range(R):
-            b0(0, r)
-        for g in range(G):
-            q("C", g * 2048, (g + 1) * 2048)
-        sh(1, 2)
-        qs(1, 0)
+        q("C", 0, 2048)
+        q("C", 2048, 4096)
         q("F", 0, 2048)
         q("F", 2048, 3072)
-        for r in range(R):
-            mx(0, 1, r, 1, 0, "C", 0, 512, 0, False, False)
-        for r in range(R):
-            b2(0, r)
-            mx(0, 1, r, 1, 1, "C", 512, 512, 0, False, True)
+        sh(1, 2)
+        qs(1, 0)
+        for r in order:
+            b1(0, r, False)
+        for r in order:
+            b2(0, r, True)
             ev(0, 1, r)
-            if r % 2:
-                st(0, 1, r - 1, r + 1)
+        st(0, 1, 0, 4)
         for r in range(3):
             b0(1, r)
             b2c(1, r)

from contextlib import ExitStack

import concourse.mybir as mybir
from concourse.masks import make_identity

F32 = mybir.dt.float32
BF16 = mybir.dt.bfloat16
U32 = mybir.dt.uint32
U8 = mybir.dt.uint8
FP8X4 = mybir.dt.float8_e4m3fn_x4
ADD = mybir.AluOpType.add

B, S, D, P, H = 2, 512, 1024, 128, 8
R = 4
G = 2
W = D // 2
FLOPS = 2 * B * S * D * P * 16


def tile_multiheadhomogeneousattention_pa_kernel(tc, x, w_now, w_back1, w_back2, bias, out):
    nc = tc.nc
    with ExitStack() as ctx:
        const = ctx.enter_context(tc.tile_pool(name="const", bufs=1))
        raw = ctx.enter_context(tc.tile_pool(name="raw", bufs=1))
        srt = ctx.enter_context(tc.tile_pool(name="srt", bufs=1))
        grp = ctx.enter_context(tc.tile_pool(name="grp", bufs=1))
        mxp = ctx.enter_context(tc.tile_pool(name="mxp", bufs=1))
        outp = ctx.enter_context(tc.tile_pool(name="outp", bufs=1))
        psum = ctx.enter_context(tc.psum_pool(name="psum", bufs=4))
        ctx.enter_context(tc.manual_schedule())

        ident = const.tile([P, P], F32, name="ident")
        ones = const.tile([P, P], BF16, name="ones")
        warm = const.tile([P, 512], BF16, name="warm")
        bias_in = const.tile([1, H * P], BF16, name="bias_in")
        bias_row = const.tile([P, H * P], BF16, name="bias_row")
        bias_all = const.tile([P, H * P], F32, name="bias_all")
        heads = {"A": 4, "B": 4, "C": 4, "E": 1, "F": 3}
        t_raw, t_srt, t_grp, t_code, t_scale = {}, {}, {}, {}, {}
        for k in ("A", "E", "B", "C", "F", 0, 1):
            nh = heads.get(k, R)
            t_raw[k] = raw.tile([P, nh * D], BF16, name="raw_%s" % k)
            t_grp[k] = grp.tile([P, nh * D], BF16, name="grp_%s" % k, align_bytes=64)
            t_code[k] = mxp.tile([P, nh * D // 4], U32, name="code_%s" % k, align_bytes=64)
            t_scale[k] = mxp.tile([P, nh * D // 4], U8, name="scale_%s" % k, align_bytes=64)
        s_grp, s_code, s_scale = [], [], []
        o_sb = []
        for n in range(B):
            s_grp.append(grp.tile([P, 2 * D], BF16, name="s_grp%d" % n, align_bytes=64))
            s_code.append(mxp.tile([P, 2 * D // 4], U32, name="s_code%d" % n, align_bytes=64))
            s_scale.append(mxp.tile([P, 2 * D // 4], U8, name="s_scale%d" % n, align_bytes=64))
            o_sb.append([outp.tile([P, 4 * R * P], F32, name="o_sb%d_%d" % (n, hf)) for hf in range(2)])

        def load_w(k, src, h0, h1):
            nc.sync.dma_start(
                out=t_raw[k][:, h0 * D:h1 * D].rearrange("p (h d) -> p h d", h=h1 - h0),
                in_=src.rearrange("h p d -> p h d"),
            )

        def load_x(n, r0, r1):
            nc.sync.dma_start(
                out=t_raw[n][:, r0 * D:r1 * D],
                in_=x[n].rearrange("(m r) d -> m (r d)", r=R)[:, r0 * D:r1 * D],
            )

        load_w("A", w_now[0:1], 0, 1)
        load_w("A", w_now[1:2], 1, 2)
        load_w("A", w_now[2:3], 2, 3)
        load_w("A", w_now[3:4], 3, 4)
        nc.sync.dma_start(out=bias_in[:], in_=bias.rearrange("(o h) p -> o (h p)", o=1))
        load_x(0, 0, 1)
        load_x(0, 1, 2)
        load_x(0, 2, 4)
        load_w("E", w_back1[0:1], 0, 1)
        load_x(1, 0, 2)
        load_x(1, 2, 4)
        load_w("B", w_now[4:6], 0, 2)
        load_w("B", w_now[6:8], 2, 4)
        load_w("C", w_back1[1:3], 0, 2)
        load_w("C", w_back1[3:5], 2, 4)
        load_w("F", w_back2[0:3], 0, 3)

        make_identity(nc, ident[:])
        nc.vector.memset(warm[:], 0.0)
        nc.vector.memset(ones[:], 1.0)
        nc.vector.memset(bias_row[:], 0.0)
        for n in range(B):
            first = s_grp[n][:].rearrange("q (t g c) -> q t g c", t=2, g=G)[:, :, :, 0:4]
            nc.vector.memset(first, 0.0)

        flipped = {}
        accs = {}

        def copy_on(eng, dst, src):
            if eng == "v":
                nc.vector.tensor_copy(out=dst, in_=src)
            else:
                nc.scalar.copy(out=dst, in_=src)

        def spread_bias():
            for hf in range(2):
                bb = psum.tile([P, 512], F32, name="bb", tag="bank")
                nc.tensor.matmul(bb[:], lhsT=ones[:], rhs=bias_row[:, hf * 512:(hf + 1) * 512], start=True, stop=True)
                nc.scalar.copy(out=bias_all[:, hf * 512:(hf + 1) * 512], in_=bb[:])

        def so(k, j0, j1, eng):
            nj = j1 - j0
            tile = srt.tile([P, nj * W], F32, name="srt_%s_%d" % (k, j0))
            for j in range(j0, j1):
                t_srt[(k, j)] = tile[:, (j - j0) * W:(j - j0 + 1) * W]
            copy_on(
                eng,
                tile[:].rearrange("p (g u q) -> p g u q", g=nj * G, u=2),
                t_raw[k][:].bitcast(F32)[:, j0 * W:j1 * W].rearrange("p (g q u) -> p g u q", g=nj * G, u=2),
            )

        def tr(k, j, dummies=0):
            bank = psum.tile([P, 512], F32, name="bank", tag="bank")
            for i in range(dummies):
                nc.tensor.matmul(bank[:], lhsT=warm[:, 0:P], rhs=warm[:], start=True, stop=True)
            for c in range(4):
                g, u = divmod(c, 2)
                if (k, j) in t_srt:
                    words = t_srt[(k, j)][:, c * P:(c + 1) * P]
                else:
                    words = t_raw[k][:].bitcast(F32)[:, j * W + g * 256 + u:j * W + (g + 1) * 256:2]
                nc.tensor.transpose(bank[:, c * P:(c + 1) * P], words, ident[:])
            flipped[(k, j)] = bank[:].rearrange("q (g u m) -> q g m u", g=G, u=2)

        def cp(k, j, eng):
            words = t_grp[k][:].bitcast(F32)
            if k in heads:
                dst = words.rearrange("q (g h m u) -> q g h m u", g=G, h=heads[k], u=2)[:, :, j, :, :]
            else:
                dst = words[:, j * W:(j + 1) * W].rearrange("q (g m u) -> q g m u", g=G, u=2)
            copy_on(eng, dst, flipped[(k, j)])

        def sh(n, r):
            nc.vector.tensor_copy(
                out=s_grp[n][:].rearrange("q (t g c) -> q t g c", t=2, g=G)[:, r - 2, :, 4:512],
                in_=t_grp[n][:].rearrange("q (t g c) -> q t g c", t=R, g=G)[:, r, :, 0:508],
            )

        def quant(src, code, scale, c0, c1):
            nc.vector.quantize_mx(
                out=code[:, c0 // 4:c1 // 4].bitcast(FP8X4),
                scales=scale[:, c0 // 4:c1 // 4],
                in_=src[:, c0:c1],
            )

        def q(k, c0, c1):
            quant(t_grp[k], t_code[k], t_scale[k], c0, c1)

        def qs(n, t):
            quant(s_grp[n], s_code[n], s_scale[n], t * D, (t + 1) * D)

        def stat(n, r, j, g):
            rr = r - j
            if rr >= 0:
                c = (rr * G + g) * P
                return t_code[n][:, c:c + P].bitcast(FP8X4), t_scale[n][:, c:c + P]
            c = ((rr + 2) * G + g) * P
            return s_code[n][:, c:c + P].bitcast(FP8X4), s_scale[n][:, c:c + P]

        def mx(n, hf, r, j, g, k, c0, width, o0, start, stop):
            if start:
                accs[(n, hf, r)] = psum.tile([P, 512], F32, name="acc", tag="acc")
            lt, ls = stat(n, r, j, g)
            nc.tensor.matmul_mx(
                out=accs[(n, hf, r)][:, o0:o0 + width],
                lhsT=lt,
                lhsT_scale=ls,
                rhs=t_code[k][:, c0:c0 + width].bitcast(FP8X4),
                rhs_scale=t_scale[k][:, c0:c0 + width],
                start=start,
                stop=stop,
            )

        span = {0: (0, 0, 4), 1: (1, 0, 4), 2: (1, 0, 2), 3: (1, 2, 2)}

        def ev(n, hf, r):
            hb, h0, nh = span[hf]
            nc.vector.tensor_tensor(
                out=o_sb[n][hb][:].rearrange("q (h r p) -> q h r p", h=4, r=R)[:, h0:h0 + nh, r, :],
                in0=accs[(n, hf, r)][:, h0 * P:(h0 + nh) * P].rearrange("q (h p) -> q h p", h=nh),
                in1=bias_all[:, (4 * hb + h0) * P:(4 * hb + h0 + nh) * P].rearrange("q (h p) -> q h p", h=nh),
                op=ADD,
            )

        def st(n, hf, r0, r1):
            hb, h0, nh = span[hf]
            nc.sync.dma_start(
                out=out[n, 4 * hb + h0:4 * hb + h0 + nh].rearrange("h (m r) p -> m h r p", r=R)[:, :, r0:r1, :],
                in_=o_sb[n][hb][:].rearrange("q (h r p) -> q h r p", h=4, r=R)[:, h0:h0 + nh, r0:r1, :],
            )

        def a0(n, r):
            mx(n, 0, r, 0, 0, "A", 0, 512, 0, True, False)
            mx(n, 0, r, 0, 1, "A", 512, 512, 0, False, False)

        def a1(n, r):
            mx(n, 0, r, 1, 0, "E", 0, 128, 384, False, False)
            mx(n, 0, r, 1, 1, "E", 128, 128, 384, False, True)

        def b0(n, r):
            mx(n, 1, r, 0, 0, "B", 0, 512, 0, True, False)
            mx(n, 1, r, 0, 1, "B", 512, 512, 0, False, False)

        def b1(n, r, stop):
            mx(n, 1, r, 1, 0, "C", 0, 512, 0, False, False)
            mx(n, 1, r, 1, 1, "C", 512, 512, 0, False, stop)

        def b2(n, r, stop=False):
            mx(n, 1, r, 2, 0, "F", 0, 128, 128, False, False)
            mx(n, 1, r, 2, 0, "F", 128, 256, 256, False, False)
            mx(n, 1, r, 2, 1, "F", 384, 128, 128, False, False)
            mx(n, 1, r, 2, 1, "F", 512, 256, 256, False, stop)

        def b2c(n, r):
            mx(n, 1, r, 1, 0, "C", 0, 512, 0, False, False)
            b2(n, r)
            mx(n, 1, r, 1, 1, "C", 512, 512, 0, False, True)


        order = (1, 2, 3, 0)
        for h in range(4):
            tr("A", h)
            cp("A", h, "sv"[h % 2])
        tr(0, 0)
        cp(0, 0, "s")
        q("A", 0, 2048)
        tr(0, 1)
        cp(0, 1, "v")
        nc.vector.tensor_copy(out=bias_row[0:1, :], in_=bias_in[:])
        q("A", 2048, 4096)
        tr(0, 2)
        cp(0, 2, "s")
        q(0, 0, 2048)
        tr(0, 3)
        cp(0, 3, "v")
        tr("E", 0)
        cp("E", 0, "s")
        q(0, 2048, 4096)
        sh(0, 3)
        q("E", 0, D)
        spread_bias()
        qs(0, 1)
        for r in range(R):
            tr(1, r)
            cp(1, r, "s")
        so("B", 0, 2, "s")
        so("B", 2, 4, "s")
        q(1, 0, 2048)
        q(1, 2048, 4096)
        sh(1, 3)
        qs(1, 1)
        for r in order:
            a0(0, r)
            a1(0, r)
            ev(0, 0, r)
        st(0, 0, 0, 4)
        for h in range(4):
            tr("B", h)
            cp("B", h, "s")
        so("C", 0, 2, "s")
        so("C", 2, 4, "v")
        q("B", 0, 2048)
        q("B", 2048, 4096)
        for r in order:
            a0(1, r)
            a1(1, r)
            ev(1, 0, r)
        st(1, 0, 0, 4)
        so("F", 0, 3, "v")
        for h in range(4):
            tr("C", h)
            cp("C", h, "s")
        for r in order:
            b0(0, r)
        sh(0, 2)
        qs(0, 0)
        for h in range(3):
            tr("F", h)
            cp("F", h, "s")
        q("C", 0, 2048)
        q("C", 2048, 4096)
        q("F", 0, 2048)
        q("F", 2048, 3072)
        sh(1, 2)
        qs(1, 0)
        for r in order:
            b1(0, r, False)
        for r in order:
            b2(0, r, True)
            ev(0, 1, r)
        st(0, 1, 0, 4)
        for r in range(3):
            b0(1, r)
            b2c(1, r)
            ev(1, 1, r)
            if r == 1:
                st(1, 1, 0, 2)
        st(1, 1, 2, 3)
        for hf, c, width in ((2, 0, 128), (3, 128, 256)):
            o0 = 256 * (hf - 2)
            mx(1, hf, 3, 0, 0, "B", o0, 256, o0, True, False)
            mx(1, hf, 3, 0, 1, "B", 512 + o0, 256, o0, False, False)
            mx(1, hf, 3, 1, 0, "C", o0, 256, o0, False, False)
            mx(1, hf, 3, 2, 0, "F", c, width, 512 - 3 * 128 + c, False, False)
            mx(1, hf, 3, 2, 1, "F", 384 + c, width, 512 - 3 * 128 + c, False, False)
            mx(1, hf, 3, 1, 1, "C", 512 + o0, 256, o0, False, True)
            ev(1, hf, 3)
            st(1, hf, 3, 4)
